import numpy as np
import ml_dtypes

BF16 = ml_dtypes.bfloat16


def bf(x):
    return np.asarray(x, np.float32).astype(BF16)


def f32(x):
    return np.asarray(x, np.float32)


def f64(x):
    return np.asarray(x).astype(np.float64)


def striped(idx):
    return np.tile(idx.reshape(-1, 16).T, (8, 1))


C, F, S, N = 256, 1024, 4096, 2048
DENSITY = 0.1
EPS = 1e-5


def setup_inputs():
    return {
        "base": f32(np.random.standard_normal((C, S))),
        "x": f32(np.random.standard_normal((C, N))),
        "ln_gain": f32(1.0 + 0.1 * np.random.standard_normal((C, 1))),
        "ln_bias": f32(0.1 * np.random.standard_normal((C, 1))),
        "w1": bf(np.random.standard_normal((C, F)) / np.sqrt(DENSITY * C)),
        "mask1": bf(np.random.uniform(size=(C, F)) < DENSITY),
        "b1": f32(0.1 * np.random.standard_normal((F, 1))),
        "w2": bf(np.random.standard_normal((F, C)) * np.sqrt(2.0 / F)),
        "b2": f32(0.1 * np.random.standard_normal((C, 1))),
        "offs": striped(np.random.permutation(S)[:N]),
    }


def reference(base, x, ln_gain, ln_bias, w1, mask1, b1, w2, b2, offs):
    idx = offs[:16].T.reshape(-1)
    xv = f64(x)
    mu = xv.mean(axis=0, keepdims=True)
    var = ((xv - mu) ** 2).mean(axis=0, keepdims=True)
    z = (xv - mu) / np.sqrt(var + EPS) * f64(ln_gain) + f64(ln_bias)
    hid = np.maximum((f64(w1) * f64(mask1)).T @ z + f64(b1), 0.0)
    y = f64(w2).T @ hid + f64(b2)
    out = f64(base).copy()
    out[:, idx] = xv + y
    return out

@@ -1,0 +1,173 @@
+import concourse.mybir as mybir
+from concourse.masks import make_identity
+
+F32 = mybir.dt.float32
+BF16 = mybir.dt.bfloat16
+U16 = mybir.dt.uint16
+ALU = mybir.AluOpType
+ACT = mybir.ActivationFunctionType
+
+P = 128
+C, F, S, N = 256, 1024, 4096, 2048
+CB = C // P
+FB = F // P
+T = 512
+NT = N // T
+EPS = 1e-5
+
+FLOPS = 2 * N * C * F * 2
+
+GAIN_ROW, LN_BIAS_ROW, B2_ROW, B1_ROW = 0, CB, 2 * CB, 3 * CB
+VEC_ROWS = 3 * CB + FB
+
+
+def tile_randomsparsetransformer_kernel(
+    tc, base, x, ln_gain, ln_bias, w1, mask1, b1, w2, b2, offs, out
+):
+    nc = tc.nc
+    with tc.tile_pool(name="held", bufs=1) as held, tc.tile_pool(name="work", bufs=2) as work:
+        offsets = held.tile([P, N // 16], U16, name="offsets")
+        nc.sync.dma_start(offsets[:], offs)
+
+        x_sb = [held.tile([P, N], F32, name=f"x{cb}") for cb in range(CB)]
+        queue = [nc.sync, nc.scalar]
+
+        def load_x_chunk(t):
+            for cb in range(CB):
+                queue[cb].dma_start(
+                    x_sb[cb][:, t * T : (t + 1) * T], x[cb * P : (cb + 1) * P, t * T : (t + 1) * T]
+                )
+
+        load_x_chunk(0)
+
+        vec_rows = held.tile([P, P], F32, name="vec_rows")
+        nc.vector.memset(vec_rows[:], 0.0)
+        for k, (row, vec) in enumerate(
+            ((GAIN_ROW, ln_gain), (LN_BIAS_ROW, ln_bias), (B2_ROW, b2), (B1_ROW, b1))
+        ):
+            rows = vec.shape[0] // P
+            queue[k % 2].dma_start(
+                vec_rows[row : row + rows, :], vec.rearrange("(r p) o -> r (p o)", p=P)
+            )
+
+        w1_sb = held.tile([P, CB, F], BF16, name="w1_sb")
+        mask_sb = held.tile([P, CB, F], BF16, name="mask_sb")
+        nc.sync.dma_start(w1_sb[:], w1.rearrange("(cb p) f -> p cb f", p=P))
+        nc.scalar.dma_start(mask_sb[:], mask1.rearrange("(cb p) f -> p cb f", p=P))
+        for t in range(1, NT):
+            load_x_chunk(t)
+        w2_sb = held.tile([P, FB, C], BF16, name="w2_sb")
+        nc.sync.dma_start(w2_sb[:], w2.rearrange("(fb p) c -> p fb c", p=P))
+        window = [held.tile([P, S], F32, name=f"window{cb}") for cb in range(CB)]
+        for cb in range(CB):
+            queue[cb].dma_start(window[cb][:], base[cb * P : (cb + 1) * P, :])
+
+        identity = held.tile([P, P], F32, name="identity")
+        make_identity(nc, identity[:])
+        mean_w = held.tile([P, P], F32, name="mean_w")
+        nc.vector.memset(mean_w[:], 1.0 / C)
+        eps_col = held.tile([P, 1], F32, name="eps_col")
+        nc.vector.memset(eps_col[:], EPS)
+
+        vec_cols = held.tile([P, VEC_ROWS], F32, name="vec_cols")
+        with tc.psum_pool(name="setup_ps", bufs=1) as setup_ps:
+            vec_ps = setup_ps.tile([P, P], F32, name="vec_ps")
+            nc.tensor.transpose(vec_ps[:], vec_rows[:], identity[:])
+            nc.vector.tensor_copy(vec_cols[:], vec_ps[:, :VEC_ROWS])
+
+        def column(row):
+            return vec_cols[:, row : row + 1]
+
+        w1m = held.tile([P, CB, F], BF16, name="w1m")
+        for cb in range(CB):
+            nc.vector.tensor_tensor(w1m[:, cb, :], w1_sb[:, cb, :], mask_sb[:, cb, :], ALU.mult)
+
+        hid = [held.tile([P, N], BF16, name=f"hid{fb}") for fb in range(FB)]
+        y_sb = [held.tile([P, N], F32, name=f"y{cb}") for cb in range(CB)]
+
+        with (
+            tc.psum_pool(name="y_pool", bufs=2) as y_pool,
+            tc.psum_pool(name="stat_pool", bufs=2) as stat_pool,
+            tc.psum_pool(name="hid_pool", bufs=4) as hid_pool,
+        ):
+
+            def layer_norm(t):
+                chunk = slice(t * T, (t + 1) * T)
+                x_sum = work.tile([P, T], F32, name="x_sum")
+                nc.vector.tensor_tensor(x_sum[:], x_sb[0][:, chunk], x_sb[1][:, chunk], ALU.add)
+                mean = stat_pool.tile([P, T], F32, name="stat")
+                nc.tensor.matmul(mean[:], mean_w[:], x_sum[:], start=True, stop=True)
+
+                centred = [work.tile([P, T], F32, name=f"centred{cb}") for cb in range(CB)]
+                square = [work.tile([P, T], F32, name=f"square{cb}") for cb in range(CB)]
+                for cb in range(CB):
+                    nc.vector.tensor_tensor(centred[cb][:], x_sb[cb][:, chunk], mean[:], ALU.subtract)
+                    nc.scalar.activation(square[cb][:], centred[cb][:], ACT.Square)
+                square_sum = work.tile([P, T], F32, name="square_sum")
+                nc.vector.tensor_tensor(square_sum[:], square[0][:], square[1][:], ALU.add)
+                var = stat_pool.tile([P, T], F32, name="stat")
+                nc.tensor.matmul(var[:], mean_w[:], square_sum[:], start=True, stop=True)
+
+                rstd = work.tile([P, T], F32, name="rstd")
+                nc.scalar.activation(rstd[:], var[:], ACT.Abs_reciprocal_sqrt, bias=eps_col[:])
+                z = [work.tile([P, T], BF16, name=f"z{cb}") for cb in range(CB)]
+                for cb in range(CB):
+                    normed = work.tile([P, T], F32, name="normed")
+                    nc.vector.tensor_tensor(normed[:], centred[cb][:], rstd[:], ALU.mult)
+                    nc.scalar.activation(
+                        z[cb][:],
+                        normed[:],
+                        ACT.Identity,
+                        scale=column(GAIN_ROW + cb),
+                        bias=column(LN_BIAS_ROW + cb),
+                    )
+                return z
+
+            def first_layer(t, z):
+                chunk = slice(t * T, (t + 1) * T)
+                for fb in range(FB):
+                    hid_ps = hid_pool.tile([P, T], F32, name="hid_ps")
+                    for cb in range(CB):
+                        nc.tensor.matmul(
+                            hid_ps[:],
+                            w1m[:, cb, fb * P : (fb + 1) * P],
+                            z[cb][:],
+                            start=(cb == 0),
+                            stop=(cb == CB - 1),
+                        )
+                    if fb % 2 == 0:
+                        nc.scalar.activation(
+                            hid[fb][:, chunk], hid_ps[:], ACT.Relu, bias=column(B1_ROW + fb)
+                        )
+                    else:
+                        nc.vector.tensor_scalar(
+                            hid[fb][:, chunk], hid_ps[:], column(B1_ROW + fb), 0.0, ALU.add, ALU.max
+                        )
+
+            def second_layer(cb, t):
+                chunk = slice(t * T, (t + 1) * T)
+                y_ps = y_pool.tile([P, T], F32, name="y_ps")
+                for fb in range(FB):
+                    nc.tensor.matmul(
+                        y_ps[:],
+                        w2_sb[:, fb, cb * P : (cb + 1) * P],
+                        hid[fb][:, chunk],
+                        start=(fb == 0),
+                        stop=(fb == FB - 1),
+                    )
+                nc.scalar.activation(y_sb[cb][:, chunk], y_ps[:], ACT.Identity, bias=column(B2_ROW + cb))
+
+            z_next = layer_norm(0)
+            for t in range(NT):
+                z = z_next
+                if t + 1 < NT:
+                    z_next = layer_norm(t + 1)
+                first_layer(t, z)
+
+            for cb in range(CB):
+                for t in range(NT):
+                    second_layer(cb, t)
+                nc.vector.tensor_tensor(
+                    window[cb][:].indirect(offsets[:]), x_sb[cb][:], y_sb[cb][:], ALU.add
+                )
+                nc.sync.dma_start(out[cb * P : (cb + 1) * P, :], window[cb][:])

@@ -11,13 +11,18 @@ P = 128
 C, F, S, N = 256, 1024, 4096, 2048
 CB = C // P
 FB = F // P
-T = 512
-NT = N // T
+BANK = 512
 EPS = 1e-5
 
 FLOPS = 2 * N * C * F * 2
 
-GAIN_ROW, LN_BIAS_ROW, B2_ROW, B1_ROW = 0, CB, 2 * CB, 3 * CB
+WIDTHS = [256, 256, 512, 512, 512]
+assert sum(WIDTHS) == N
+PIECES = [(sum(WIDTHS[:i]), width) for i, width in enumerate(WIDTHS)]
+assert all(start // BANK == (start + width - 1) // BANK for start, width in PIECES)
+IN_FLIGHT = 3
+
+GAIN_ROW, LN_BIAS_ROW, B1_ROW, B2_ROW = 0, CB, 2 * CB, 2 * CB + FB
 VEC_ROWS = 3 * CB + FB
 
 
@@ -25,65 +30,54 @@ def tile_randomsparsetransformer_kernel(
     tc, base, x, ln_gain, ln_bias, w1, mask1, b1, w2, b2, offs, out
 ):
     nc = tc.nc
-    with tc.tile_pool(name="held", bufs=1) as held, tc.tile_pool(name="work", bufs=2) as work:
+    with tc.tile_pool(name="held", bufs=1) as held, tc.tile_pool(name="work", bufs=IN_FLIGHT) as work:
+        x_piece = [held.tile([P, CB, width], F32, name=f"x_piece{i}") for i, width in enumerate(WIDTHS)]
+        z_piece = [held.tile([P, CB, width], BF16, name=f"z_piece{i}") for i, width in enumerate(WIDTHS)]
+        x_whole = [held.tile([P, N], F32, name=f"x_whole{cb}") for cb in range(CB)]
+        y_whole = [held.tile([P, N], F32, name=f"y_whole{cb}") for cb in range(CB)]
+        window = [held.tile([P, S], F32, name=f"window{cb}") for cb in range(CB)]
         offsets = held.tile([P, N // 16], U16, name="offsets")
-        nc.sync.dma_start(offsets[:], offs)
-
-        x_sb = [held.tile([P, N], F32, name=f"x{cb}") for cb in range(CB)]
-        queue = [nc.sync, nc.scalar]
-
-        def load_x_chunk(t):
-            for cb in range(CB):
-                queue[cb].dma_start(
-                    x_sb[cb][:, t * T : (t + 1) * T], x[cb * P : (cb + 1) * P, t * T : (t + 1) * T]
-                )
-
-        load_x_chunk(0)
-
-        vec_rows = held.tile([P, P], F32, name="vec_rows")
-        nc.vector.memset(vec_rows[:], 0.0)
-        for k, (row, vec) in enumerate(
-            ((GAIN_ROW, ln_gain), (LN_BIAS_ROW, ln_bias), (B2_ROW, b2), (B1_ROW, b1))
-        ):
-            rows = vec.shape[0] // P
-            queue[k % 2].dma_start(
-                vec_rows[row : row + rows, :], vec.rearrange("(r p) o -> r (p o)", p=P)
-            )
-
+        hid = [[held.tile([P, BANK], BF16, name=f"hid{t}_{fb}") for fb in range(FB)] for t in range(N // BANK)]
         w1_sb = held.tile([P, CB, F], BF16, name="w1_sb")
         mask_sb = held.tile([P, CB, F], BF16, name="mask_sb")
-        nc.sync.dma_start(w1_sb[:], w1.rearrange("(cb p) f -> p cb f", p=P))
-        nc.scalar.dma_start(mask_sb[:], mask1.rearrange("(cb p) f -> p cb f", p=P))
-        for t in range(1, NT):
-            load_x_chunk(t)
+        w1m = held.tile([P, CB, F], BF16, name="w1m")
         w2_sb = held.tile([P, FB, C], BF16, name="w2_sb")
-        nc.sync.dma_start(w2_sb[:], w2.rearrange("(fb p) c -> p fb c", p=P))
-        window = [held.tile([P, S], F32, name=f"window{cb}") for cb in range(CB)]
-        for cb in range(CB):
-            queue[cb].dma_start(window[cb][:], base[cb * P : (cb + 1) * P, :])
-
-        identity = held.tile([P, P], F32, name="identity")
-        make_identity(nc, identity[:])
-        mean_w = held.tile([P, P], F32, name="mean_w")
-        nc.vector.memset(mean_w[:], 1.0 / C)
-        eps_col = held.tile([P, 1], F32, name="eps_col")
-        nc.vector.memset(eps_col[:], EPS)
-
+        vec_rows = held.tile([P, P], F32, name="vec_rows")
         vec_cols = held.tile([P, VEC_ROWS], F32, name="vec_cols")
-        with tc.psum_pool(name="setup_ps", bufs=1) as setup_ps:
-            vec_ps = setup_ps.tile([P, P], F32, name="vec_ps")
-            nc.tensor.transpose(vec_ps[:], vec_rows[:], identity[:])
-            nc.vector.tensor_copy(vec_cols[:], vec_ps[:, :VEC_ROWS])
+        identity = held.tile([P, P], F32, name="identity")
+        mean_w = held.tile([P, P], F32, name="mean_w")
+        eps_col = held.tile([P, 1], F32, name="eps_col")
+
+        nc.vector.memset(vec_rows[:], 0.0)
+        nc.vector.memset(mean_w[:], 1.0 / C)
+        nc.vector.memset(eps_col[:], EPS)
+        make_identity(nc, identity[:])
+
+        x_blocks = x.rearrange("(cb p) n -> p cb n", p=P)
+
+        def load_x_piece(i):
+            start, width = PIECES[i]
+            nc.sync.dma_start(x_piece[i][:], x_blocks[:, :, start : start + width])
+
+        for i in range(IN_FLIGHT):
+            load_x_piece(i)
+        nc.sync.dma_start(w1_sb[:], w1.rearrange("(cb p) f -> p cb f", p=P))
+        nc.sync.dma_start(mask_sb[:], mask1.rearrange("(cb p) f -> p cb f", p=P))
+        for i in range(IN_FLIGHT, len(PIECES)):
+            load_x_piece(i)
+        nc.sync.dma_start(w2_sb[:], w2.rearrange("(fb p) c -> p fb c", p=P))
+        nc.sync.dma_start(offsets[:], offs)
+        for cb in range(CB):
+            nc.sync.dma_start(x_whole[cb][:], x[cb * P : (cb + 1) * P, :])
+        for cb in range(CB):
+            nc.sync.dma_start(window[cb][:], base[cb * P : (cb + 1) * P, :])
+
+        for row, vec in ((GAIN_ROW, ln_gain), (LN_BIAS_ROW, ln_bias), (B1_ROW, b1), (B2_ROW, b2)):
+            rows = vec.shape[0] // P
+            nc.scalar.dma_start(vec_rows[row : row + rows, :], vec.rearrange("(r p) o -> r (p o)", p=P))
 
         def column(row):
             return vec_cols[:, row : row + 1]
-
-        w1m = held.tile([P, CB, F], BF16, name="w1m")
-        for cb in range(CB):
-            nc.vector.tensor_tensor(w1m[:, cb, :], w1_sb[:, cb, :], mask_sb[:, cb, :], ALU.mult)
-
-        hid = [held.tile([P, N], BF16, name=f"hid{fb}") for fb in range(FB)]
-        y_sb = [held.tile([P, N], F32, name=f"y{cb}") for cb in range(CB)]
 
         with (
             tc.psum_pool(name="y_pool", bufs=2) as y_pool,
@@ -91,83 +85,92 @@ def tile_randomsparsetransformer_kernel(
             tc.psum_pool(name="hid_pool", bufs=4) as hid_pool,
         ):
 
-            def layer_norm(t):
-                chunk = slice(t * T, (t + 1) * T)
-                x_sum = work.tile([P, T], F32, name="x_sum")
-                nc.vector.tensor_tensor(x_sum[:], x_sb[0][:, chunk], x_sb[1][:, chunk], ALU.add)
-                mean = stat_pool.tile([P, T], F32, name="stat")
+            def statistics(i):
+                width = WIDTHS[i]
+                x_sum = work.tile([P, width], F32, name="x_sum")
+                nc.vector.tensor_tensor(x_sum[:], x_piece[i][:, 0, :], x_piece[i][:, 1, :], ALU.add)
+                mean = stat_pool.tile([P, width], F32, name="mean", tag="stat")
                 nc.tensor.matmul(mean[:], mean_w[:], x_sum[:], start=True, stop=True)
 
-                centred = [work.tile([P, T], F32, name=f"centred{cb}") for cb in range(CB)]
-                square = [work.tile([P, T], F32, name=f"square{cb}") for cb in range(CB)]
+                centred = [work.tile([P, width], F32, name=f"centred{cb}") for cb in range(CB)]
+                square = [work.tile([P, width], F32, name=f"square{cb}") for cb in range(CB)]
                 for cb in range(CB):
-                    nc.vector.tensor_tensor(centred[cb][:], x_sb[cb][:, chunk], mean[:], ALU.subtract)
+                    nc.vector.tensor_tensor(centred[cb][:], x_piece[i][:, cb, :], mean[:], ALU.subtract)
                     nc.scalar.activation(square[cb][:], centred[cb][:], ACT.Square)
-                square_sum = work.tile([P, T], F32, name="square_sum")
+                square_sum = work.tile([P, width], F32, name="square_sum")
                 nc.vector.tensor_tensor(square_sum[:], square[0][:], square[1][:], ALU.add)
-                var = stat_pool.tile([P, T], F32, name="stat")
+                var = stat_pool.tile([P, width], F32, name="var", tag="stat")
                 nc.tensor.matmul(var[:], mean_w[:], square_sum[:], start=True, stop=True)
-
-                rstd = work.tile([P, T], F32, name="rstd")
+                rstd = work.tile([P, width], F32, name="rstd")
                 nc.scalar.activation(rstd[:], var[:], ACT.Abs_reciprocal_sqrt, bias=eps_col[:])
-                z = [work.tile([P, T], BF16, name=f"z{cb}") for cb in range(CB)]
+                return centred, rstd
+
+            def normalise(i, centred, rstd):
                 for cb in range(CB):
-                    normed = work.tile([P, T], F32, name="normed")
+                    normed = work.tile([P, WIDTHS[i]], F32, name=f"normed{cb}")
                     nc.vector.tensor_tensor(normed[:], centred[cb][:], rstd[:], ALU.mult)
                     nc.scalar.activation(
-                        z[cb][:],
+                        z_piece[i][:, cb, :],
                         normed[:],
                         ACT.Identity,
                         scale=column(GAIN_ROW + cb),
                         bias=column(LN_BIAS_ROW + cb),
                     )
-                return z
 
-            def first_layer(t, z):
-                chunk = slice(t * T, (t + 1) * T)
+            def first_layer(i):
+                start, width = PIECES[i]
+                t, first = divmod(start, BANK)
                 for fb in range(FB):
-                    hid_ps = hid_pool.tile([P, T], F32, name="hid_ps")
+                    hid_ps = hid_pool.tile([P, width], F32, name="hid_ps")
                     for cb in range(CB):
                         nc.tensor.matmul(
                             hid_ps[:],
                             w1m[:, cb, fb * P : (fb + 1) * P],
-                            z[cb][:],
+                            z_piece[i][:, cb, :],
                             start=(cb == 0),
                             stop=(cb == CB - 1),
                         )
+                    hid_out = hid[t][fb][:, first : first + width]
                     if fb % 2 == 0:
-                        nc.scalar.activation(
-                            hid[fb][:, chunk], hid_ps[:], ACT.Relu, bias=column(B1_ROW + fb)
-                        )
+                        nc.scalar.activation(hid_out, hid_ps[:], ACT.Relu, bias=column(B1_ROW + fb))
                     else:
-                        nc.vector.tensor_scalar(
-                            hid[fb][:, chunk], hid_ps[:], column(B1_ROW + fb), 0.0, ALU.add, ALU.max
-                        )
+                        nc.vector.tensor_scalar(hid_out, hid_ps[:], column(B1_ROW + fb), 0.0, ALU.add, ALU.max)
 
             def second_layer(cb, t):
-                chunk = slice(t * T, (t + 1) * T)
-                y_ps = y_pool.tile([P, T], F32, name="y_ps")
+                y_ps = y_pool.tile([P, BANK], F32, name="y_ps")
                 for fb in range(FB):
                     nc.tensor.matmul(
                         y_ps[:],
                         w2_sb[:, fb, cb * P : (cb + 1) * P],
-                        hid[fb][:, chunk],
+                        hid[t][fb][:],
                         start=(fb == 0),
                         stop=(fb == FB - 1),
                     )
-                nc.scalar.activation(y_sb[cb][:, chunk], y_ps[:], ACT.Identity, bias=column(B2_ROW + cb))
-
-            z_next = layer_norm(0)
-            for t in range(NT):
-                z = z_next
-                if t + 1 < NT:
-                    z_next = layer_norm(t + 1)
-                first_layer(t, z)
-
-            for cb in range(CB):
-                for t in range(NT):
-                    second_layer(cb, t)
-                nc.vector.tensor_tensor(
-                    window[cb][:].indirect(offsets[:]), x_sb[cb][:], y_sb[cb][:], ALU.add
+                nc.scalar.activation(
+                    y_whole[cb][:, t * BANK : (t + 1) * BANK], y_ps[:], ACT.Identity, bias=column(B2_ROW + cb)
                 )
+
+            stats = [statistics(i) for i in range(IN_FLIGHT)]
+            vec_ps = y_pool.tile([P, P], F32, name="vec_ps", tag="y_ps")
+            nc.tensor.transpose(vec_ps[:], vec_rows[:], identity[:])
+            nc.vector.tensor_copy(vec_cols[:], vec_ps[:, :VEC_ROWS])
+            normalise(0, *stats[0])
+            for cb in range(CB):
+                nc.vector.tensor_tensor(w1m[:, cb, :], w1_sb[:, cb, :], mask_sb[:, cb, :], ALU.mult)
+            for i in range(1, IN_FLIGHT):
+                normalise(i, *stats[i])
+            for i in range(IN_FLIGHT, len(PIECES)):
+                normalise(i, *statistics(i))
+
+            def scatter(cb):
+                nc.vector.tensor_tensor(window[cb][:].indirect(offsets[:]), x_whole[cb][:], y_whole[cb][:], ALU.add)
                 nc.sync.dma_start(out[cb * P : (cb + 1) * P, :], window[cb][:])
+
+            for i, (start, width) in enumerate(PIECES):
+                first_layer(i)
+                if (start + width) % BANK == 0:
+                    second_layer(0, start // BANK)
+            scatter(0)
+            for t in range(N // BANK):
+                second_layer(1, t)
+            scatter(1)

@@ -80,9 +80,9 @@ def tile_randomsparsetransformer_kernel(
             return vec_cols[:, row : row + 1]
 
         with (
-            tc.psum_pool(name="y_pool", bufs=2) as y_pool,
+            tc.psum_pool(name="y_pool", bufs=1) as y_pool,
             tc.psum_pool(name="stat_pool", bufs=2) as stat_pool,
-            tc.psum_pool(name="hid_pool", bufs=4) as hid_pool,
+            tc.psum_pool(name="hid_pool", bufs=5) as hid_pool,
         ):
 
             def statistics(i):

@@ -80,9 +80,9 @@ def tile_randomsparsetransformer_kernel(
             return vec_cols[:, row : row + 1]
 
         with (
-            tc.psum_pool(name="y_pool", bufs=1) as y_pool,
+            tc.psum_pool(name="y_pool", bufs=2) as y_pool,
             tc.psum_pool(name="stat_pool", bufs=2) as stat_pool,
-            tc.psum_pool(name="hid_pool", bufs=5) as hid_pool,
+            tc.psum_pool(name="hid_pool", bufs=4) as hid_pool,
         ):
 
             def statistics(i):
@@ -109,12 +109,13 @@ def tile_randomsparsetransformer_kernel(
                 for cb in range(CB):
                     normed = work.tile([P, WIDTHS[i]], F32, name=f"normed{cb}")
                     nc.vector.tensor_tensor(normed[:], centred[cb][:], rstd[:], ALU.mult)
-                    nc.scalar.activation(
+                    nc.vector.tensor_scalar(
                         z_piece[i][:, cb, :],
                         normed[:],
-                        ACT.Identity,
-                        scale=column(GAIN_ROW + cb),
-                        bias=column(LN_BIAS_ROW + cb),
+                        column(GAIN_ROW + cb),
+                        column(LN_BIAS_ROW + cb),
+                        ALU.mult,
+                        ALU.add,
                     )
 
             def first_layer(i):
@@ -131,7 +132,7 @@ def tile_randomsparsetransformer_kernel(
                             stop=(cb == CB - 1),
                         )
                     hid_out = hid[t][fb][:, first : first + width]
-                    if fb % 2 == 0:
+                    if fb % 3 != 1:
                         nc.scalar.activation(hid_out, hid_ps[:], ACT.Relu, bias=column(B1_ROW + fb))
                     else:
                         nc.vector.tensor_scalar(hid_out, hid_ps[:], column(B1_ROW + fb), 0.0, ALU.add, ALU.max)

@@ -16,7 +16,11 @@ EPS = 1e-5
 
 FLOPS = 2 * N * C * F * 2
 
-WIDTHS = [256, 256, 512, 512, 512]
+TB = BANK // C
+UNIT = TB * P
+UNITS = N // UNIT
+
+WIDTHS = [UNIT, UNIT, BANK, BANK, BANK]
 assert sum(WIDTHS) == N
 PIECES = [(sum(WIDTHS[:i]), width) for i, width in enumerate(WIDTHS)]
 assert all(start // BANK == (start + width - 1) // BANK for start, width in PIECES)
@@ -31,7 +35,7 @@ def tile_randomsparsetransformer_kernel(
 ):
     nc = tc.nc
     with tc.tile_pool(name="held", bufs=1) as held, tc.tile_pool(name="work", bufs=IN_FLIGHT) as work:
-        x_piece = [held.tile([P, CB, width], F32, name=f"x_piece{i}") for i, width in enumerate(WIDTHS)]
+        x_unit = [held.tile([P, CB, UNIT], F32, name=f"x_unit{u}") for u in range(UNITS)]
         z_piece = [held.tile([P, CB, width], BF16, name=f"z_piece{i}") for i, width in enumerate(WIDTHS)]
         x_whole = [held.tile([P, N], F32, name=f"x_whole{cb}") for cb in range(CB)]
         y_whole = [held.tile([P, N], F32, name=f"y_whole{cb}") for cb in range(CB)]
@@ -45,26 +49,23 @@ def tile_randomsparsetransformer_kernel(
         vec_rows = held.tile([P, P], F32, name="vec_rows")
         vec_cols = held.tile([P, VEC_ROWS], F32, name="vec_cols")
         identity = held.tile([P, P], F32, name="identity")
-        mean_w = held.tile([P, P], F32, name="mean_w")
         eps_col = held.tile([P, 1], F32, name="eps_col")
 
         nc.vector.memset(vec_rows[:], 0.0)
-        nc.vector.memset(mean_w[:], 1.0 / C)
         nc.vector.memset(eps_col[:], EPS)
         make_identity(nc, identity[:])
 
         x_blocks = x.rearrange("(cb p) n -> p cb n", p=P)
 
-        def load_x_piece(i):
-            start, width = PIECES[i]
-            nc.sync.dma_start(x_piece[i][:], x_blocks[:, :, start : start + width])
+        def load_x_unit(u):
+            nc.sync.dma_start(x_unit[u][:], x_blocks[:, :, u * UNIT : (u + 1) * UNIT])
 
-        for i in range(IN_FLIGHT):
-            load_x_piece(i)
+        for u in range(2):
+            load_x_unit(u)
         nc.sync.dma_start(w1_sb[:], w1.rearrange("(cb p) f -> p cb f", p=P))
         nc.sync.dma_start(mask_sb[:], mask1.rearrange("(cb p) f -> p cb f", p=P))
-        for i in range(IN_FLIGHT, len(PIECES)):
-            load_x_piece(i)
+        for u in range(2, UNITS):
+            load_x_unit(u)
         nc.sync.dma_start(w2_sb[:], w2.rearrange("(fb p) c -> p fb c", p=P))
         nc.sync.dma_start(offsets[:], offs)
         for cb in range(CB):
@@ -81,42 +82,63 @@ def tile_randomsparsetransformer_kernel(
 
         with (
             tc.psum_pool(name="y_pool", bufs=2) as y_pool,
-            tc.psum_pool(name="stat_pool", bufs=2) as stat_pool,
-            tc.psum_pool(name="hid_pool", bufs=4) as hid_pool,
+            tc.psum_pool(name="flip_pool", bufs=3) as flip_pool,
+            tc.psum_pool(name="hid_pool", bufs=3) as hid_pool,
         ):
 
-            def statistics(i):
-                width = WIDTHS[i]
-                x_sum = work.tile([P, width], F32, name="x_sum")
-                nc.vector.tensor_tensor(x_sum[:], x_piece[i][:, 0, :], x_piece[i][:, 1, :], ALU.add)
-                mean = stat_pool.tile([P, width], F32, name="mean", tag="stat")
-                nc.tensor.matmul(mean[:], mean_w[:], x_sum[:], start=True, stop=True)
-
-                centred = [work.tile([P, width], F32, name=f"centred{cb}") for cb in range(CB)]
-                square = [work.tile([P, width], F32, name=f"square{cb}") for cb in range(CB)]
-                for cb in range(CB):
-                    nc.vector.tensor_tensor(centred[cb][:], x_piece[i][:, cb, :], mean[:], ALU.subtract)
-                    nc.scalar.activation(square[cb][:], centred[cb][:], ACT.Square)
-                square_sum = work.tile([P, width], F32, name="square_sum")
-                nc.vector.tensor_tensor(square_sum[:], square[0][:], square[1][:], ALU.add)
-                var = stat_pool.tile([P, width], F32, name="var", tag="stat")
-                nc.tensor.matmul(var[:], mean_w[:], square_sum[:], start=True, stop=True)
-                rstd = work.tile([P, width], F32, name="rstd")
-                nc.scalar.activation(rstd[:], var[:], ACT.Abs_reciprocal_sqrt, bias=eps_col[:])
-                return centred, rstd
-
-            def normalise(i, centred, rstd):
-                for cb in range(CB):
-                    normed = work.tile([P, WIDTHS[i]], F32, name=f"normed{cb}")
-                    nc.vector.tensor_tensor(normed[:], centred[cb][:], rstd[:], ALU.mult)
+            def standardise(u):
+                x_flipped = flip_pool.tile([P, TB, C], F32, name="x_flipped", tag="flip")
+                for tb in range(TB):
+                    for cb in range(CB):
+                        nc.tensor.transpose(
+                            x_flipped[:, tb, cb * P : (cb + 1) * P],
+                            x_unit[u][:, cb, tb * P : (tb + 1) * P],
+                            identity[:],
+                        )
+                stats = work.tile([P, TB, 6], F32, name="stats")
+                mean_var = work.tile([P, TB, 2], F32, name="mean_var")
+                for tb in range(TB):
+                    nc.vector.bn_stats(stats[:, tb, :], x_flipped[:, tb, :])
+                    nc.vector.bn_aggr(mean_var[:, tb, :], stats[:, tb, :])
+                rstd = work.tile([P, TB], F32, name="rstd")
+                nc.scalar.activation(rstd[:], mean_var[:, :, 1], ACT.Abs_reciprocal_sqrt, bias=eps_col[:])
+                standard = work.tile([P, TB, C], F32, name="standard")
+                for tb in range(TB):
                     nc.vector.tensor_scalar(
-                        z_piece[i][:, cb, :],
-                        normed[:],
-                        column(GAIN_ROW + cb),
-                        column(LN_BIAS_ROW + cb),
+                        standard[:, tb, :],
+                        x_flipped[:, tb, :],
+                        mean_var[:, tb, 0:1],
+                        rstd[:, tb : tb + 1],
+                        ALU.subtract,
                         ALU.mult,
-                        ALU.add,
                     )
+                return standard
+
+            def z_columns(u, cb):
+                i = max(i for i, (start, width) in enumerate(PIECES) if start <= u * UNIT)
+                first = u * UNIT - PIECES[i][0]
+                return z_piece[i][:, cb, first : first + UNIT]
+
+            def gain_and_bias(u, standard):
+                flipped_back = flip_pool.tile([P, CB, UNIT], F32, name="flipped_back", tag="flip")
+                for cb in range(CB):
+                    for tb in range(TB):
+                        nc.tensor.transpose(
+                            flipped_back[:, cb, tb * P : (tb + 1) * P],
+                            standard[:, tb, cb * P : (cb + 1) * P],
+                            identity[:],
+                        )
+                for cb in range(CB):
+                    nc.scalar.activation(
+                        z_columns(u, cb),
+                        flipped_back[:, cb, :],
+                        ACT.Identity,
+                        bias=column(LN_BIAS_ROW + cb),
+                        scale=column(GAIN_ROW + cb),
+                    )
+
+            def layer_norm(u):
+                gain_and_bias(u, standardise(u))
 
             def first_layer(i):
                 start, width = PIECES[i]
@@ -132,7 +154,7 @@ def tile_randomsparsetransformer_kernel(
                             stop=(cb == CB - 1),
                         )
                     hid_out = hid[t][fb][:, first : first + width]
-                    if fb % 3 != 1:
+                    if fb % 4 != 3:
                         nc.scalar.activation(hid_out, hid_ps[:], ACT.Relu, bias=column(B1_ROW + fb))
                     else:
                         nc.vector.tensor_scalar(hid_out, hid_ps[:], column(B1_ROW + fb), 0.0, ALU.add, ALU.max)
@@ -151,21 +173,19 @@ def tile_randomsparsetransformer_kernel(
                     y_whole[cb][:, t * BANK : (t + 1) * BANK], y_ps[:], ACT.Identity, bias=column(B2_ROW + cb)
                 )
 
-            stats = [statistics(i) for i in range(IN_FLIGHT)]
-            vec_ps = y_pool.tile([P, P], F32, name="vec_ps", tag="y_ps")
-            nc.tensor.transpose(vec_ps[:], vec_rows[:], identity[:])
-            nc.vector.tensor_copy(vec_cols[:], vec_ps[:, :VEC_ROWS])
-            normalise(0, *stats[0])
-            for cb in range(CB):
-                nc.vector.tensor_tensor(w1m[:, cb, :], w1_sb[:, cb, :], mask_sb[:, cb, :], ALU.mult)
-            for i in range(1, IN_FLIGHT):
-                normalise(i, *stats[i])
-            for i in range(IN_FLIGHT, len(PIECES)):
-                normalise(i, *statistics(i))
-
             def scatter(cb):
                 nc.vector.tensor_tensor(window[cb][:].indirect(offsets[:]), x_whole[cb][:], y_whole[cb][:], ALU.add)
                 nc.sync.dma_start(out[cb * P : (cb + 1) * P, :], window[cb][:])
+
+            standard0 = standardise(0)
+            vec_ps = flip_pool.tile([P, P], F32, name="vec_ps", tag="flip")
+            nc.tensor.transpose(vec_ps[:], vec_rows[:], identity[:])
+            nc.vector.tensor_copy(vec_cols[:], vec_ps[:, :VEC_ROWS])
+            gain_and_bias(0, standard0)
+            for cb in range(CB):
+                nc.vector.tensor_tensor(w1m[:, cb, :], w1_sb[:, cb, :], mask_sb[:, cb, :], ALU.mult)
+            for u in range(1, UNITS):
+                layer_norm(u)
 
             for i, (start, width) in enumerate(PIECES):
                 first_layer(i)

@@ -24,7 +24,11 @@ WIDTHS = [UNIT, UNIT, BANK, BANK, BANK]
 assert sum(WIDTHS) == N
 PIECES = [(sum(WIDTHS[:i]), width) for i, width in enumerate(WIDTHS)]
 assert all(start // BANK == (start + width - 1) // BANK for start, width in PIECES)
-IN_FLIGHT = 3
+AHEAD = 2
+IN_FLIGHT = AHEAD + 2
+
+HALVES = 2
+FH = F // HALVES
 
 GAIN_ROW, LN_BIAS_ROW, B1_ROW, B2_ROW = 0, CB, 2 * CB, 2 * CB + FB
 VEC_ROWS = 3 * CB + FB
@@ -42,9 +46,9 @@ def tile_randomsparsetransformer_kernel(
         window = [held.tile([P, S], F32, name=f"window{cb}") for cb in range(CB)]
         offsets = held.tile([P, N // 16], U16, name="offsets")
         hid = [[held.tile([P, BANK], BF16, name=f"hid{t}_{fb}") for fb in range(FB)] for t in range(N // BANK)]
-        w1_sb = held.tile([P, CB, F], BF16, name="w1_sb")
-        mask_sb = held.tile([P, CB, F], BF16, name="mask_sb")
-        w1m = held.tile([P, CB, F], BF16, name="w1m")
+        w1_sb = [held.tile([P, CB, FH], BF16, name=f"w1_sb{h}") for h in range(HALVES)]
+        mask_sb = [held.tile([P, CB, FH], BF16, name=f"mask_sb{h}") for h in range(HALVES)]
+        w1m = [held.tile([P, CB, FH], BF16, name=f"w1m{h}") for h in range(HALVES)]
         w2_sb = held.tile([P, FB, C], BF16, name="w2_sb")
         vec_rows = held.tile([P, P], F32, name="vec_rows")
         vec_cols = held.tile([P, VEC_ROWS], F32, name="vec_cols")
@@ -56,14 +60,20 @@ def tile_randomsparsetransformer_kernel(
         make_identity(nc, identity[:])
 
         x_blocks = x.rearrange("(cb p) n -> p cb n", p=P)
+        w1_blocks = w1.rearrange("(cb p) f -> p cb f", p=P)
+        mask_blocks = mask1.rearrange("(cb p) f -> p cb f", p=P)
 
         def load_x_unit(u):
             nc.sync.dma_start(x_unit[u][:], x_blocks[:, :, u * UNIT : (u + 1) * UNIT])
 
-        for u in range(2):
-            load_x_unit(u)
-        nc.sync.dma_start(w1_sb[:], w1.rearrange("(cb p) f -> p cb f", p=P))
-        nc.sync.dma_start(mask_sb[:], mask1.rearrange("(cb p) f -> p cb f", p=P))
+        load_x_unit(0)
+        for row, vec in ((GAIN_ROW, ln_gain), (LN_BIAS_ROW, ln_bias), (B1_ROW, b1), (B2_ROW, b2)):
+            rows = vec.shape[0] // P
+            nc.sync.dma_start(vec_rows[row : row + rows, :], vec.rearrange("(r p) o -> r (p o)", p=P))
+        load_x_unit(1)
+        for h in range(HALVES):
+            nc.sync.dma_start(w1_sb[h][:], w1_blocks[:, :, h * FH : (h + 1) * FH])
+            nc.sync.dma_start(mask_sb[h][:], mask_blocks[:, :, h * FH : (h + 1) * FH])
         for u in range(2, UNITS):
             load_x_unit(u)
         nc.sync.dma_start(w2_sb[:], w2.rearrange("(fb p) c -> p fb c", p=P))
@@ -72,10 +82,6 @@ def tile_randomsparsetransformer_kernel(
             nc.sync.dma_start(x_whole[cb][:], x[cb * P : (cb + 1) * P, :])
         for cb in range(CB):
             nc.sync.dma_start(window[cb][:], base[cb * P : (cb + 1) * P, :])
-
-        for row, vec in ((GAIN_ROW, ln_gain), (LN_BIAS_ROW, ln_bias), (B1_ROW, b1), (B2_ROW, b2)):
-            rows = vec.shape[0] // P
-            nc.scalar.dma_start(vec_rows[row : row + rows, :], vec.rearrange("(r p) o -> r (p o)", p=P))
 
         def column(row):
             return vec_cols[:, row : row + 1]
@@ -137,18 +143,19 @@ def tile_randomsparsetransformer_kernel(
                         scale=column(GAIN_ROW + cb),
                     )
 
-            def layer_norm(u):
-                gain_and_bias(u, standardise(u))
+            def mask_weights(h):
+                nc.vector.tensor_tensor(w1m[h][:], w1_sb[h][:], mask_sb[h][:], ALU.mult)
 
-            def first_layer(i):
+            def first_layer(i, hidden_blocks):
                 start, width = PIECES[i]
                 t, first = divmod(start, BANK)
-                for fb in range(FB):
+                for fb in hidden_blocks:
+                    h, first_in_half = divmod(fb * P, FH)
                     hid_ps = hid_pool.tile([P, width], F32, name="hid_ps")
                     for cb in range(CB):
                         nc.tensor.matmul(
                             hid_ps[:],
-                            w1m[:, cb, fb * P : (fb + 1) * P],
+                            w1m[h][:, cb, first_in_half : first_in_half + P],
                             z_piece[i][:, cb, :],
                             start=(cb == 0),
                             stop=(cb == CB - 1),
@@ -177,18 +184,31 @@ def tile_randomsparsetransformer_kernel(
                 nc.vector.tensor_tensor(window[cb][:].indirect(offsets[:]), x_whole[cb][:], y_whole[cb][:], ALU.add)
                 nc.sync.dma_start(out[cb * P : (cb + 1) * P, :], window[cb][:])
 
-            standard0 = standardise(0)
-            vec_ps = flip_pool.tile([P, P], F32, name="vec_ps", tag="flip")
+            standard = {}
+
+            def norm_step(u):
+                if u < UNITS:
+                    gain_and_bias(u, standard[u])
+                if u + AHEAD < UNITS:
+                    standard[u + AHEAD] = standardise(u + AHEAD)
+
+            standard[0] = standardise(0)
+            vec_ps = y_pool.tile([P, P], F32, name="vec_ps", tag="y_ps")
             nc.tensor.transpose(vec_ps[:], vec_rows[:], identity[:])
             nc.vector.tensor_copy(vec_cols[:], vec_ps[:, :VEC_ROWS])
-            gain_and_bias(0, standard0)
-            for cb in range(CB):
-                nc.vector.tensor_tensor(w1m[:, cb, :], w1_sb[:, cb, :], mask_sb[:, cb, :], ALU.mult)
-            for u in range(1, UNITS):
-                layer_norm(u)
+            mask_weights(0)
+            standard[1] = standardise(1)
+            mask_weights(1)
+            norm_step(0)
+            norm_step(1)
 
+            next_unit = 2
             for i, (start, width) in enumerate(PIECES):
-                first_layer(i)
+                parts = width // UNIT
+                for part in range(parts):
+                    first_layer(i, range(part * FB // parts, (part + 1) * FB // parts))
+                    norm_step(next_unit)
+                    next_unit += 1
                 if (start + width) % BANK == 0:
                     second_layer(0, start // BANK)
             scatter(0)

@@ -144,7 +144,7 @@ def tile_randomsparsetransformer_kernel(
                     )
 
             def mask_weights(h):
-                nc.vector.tensor_tensor(w1m[h][:], w1_sb[h][:], mask_sb[h][:], ALU.mult)
+                nc.gpsimd.tensor_tensor(w1m[h][:], w1_sb[h][:], mask_sb[h][:], ALU.mult)
 
             def first_layer(i, hidden_blocks):
                 start, width = PIECES[i]

@@ -16,19 +16,22 @@ EPS = 1e-5
 
 FLOPS = 2 * N * C * F * 2
 
-TB = BANK // C
-UNIT = TB * P
-UNITS = N // UNIT
+WHOLE = BANK // C * P
+UNIT_WIDTHS = [P, P] + [WHOLE] * ((N - 2 * P) // WHOLE)
+assert sum(UNIT_WIDTHS) == N
+UNITS = len(UNIT_WIDTHS)
+UNIT_STARTS = [sum(UNIT_WIDTHS[:u]) for u in range(UNITS)]
 
-WIDTHS = [UNIT, UNIT, BANK, BANK, BANK]
+WIDTHS = [WHOLE, WHOLE, BANK, BANK, BANK]
 assert sum(WIDTHS) == N
 PIECES = [(sum(WIDTHS[:i]), width) for i, width in enumerate(WIDTHS)]
 assert all(start // BANK == (start + width - 1) // BANK for start, width in PIECES)
 AHEAD = 2
 IN_FLIGHT = AHEAD + 2
+STATS_AT_ONCE = 2
 
-HALVES = 2
-FH = F // HALVES
+QUARTERS = 4
+FQ = F // QUARTERS
 
 GAIN_ROW, LN_BIAS_ROW, B1_ROW, B2_ROW = 0, CB, 2 * CB, 2 * CB + FB
 VEC_ROWS = 3 * CB + FB
@@ -39,16 +42,16 @@ def tile_randomsparsetransformer_kernel(
 ):
     nc = tc.nc
     with tc.tile_pool(name="held", bufs=1) as held, tc.tile_pool(name="work", bufs=IN_FLIGHT) as work:
-        x_unit = [held.tile([P, CB, UNIT], F32, name=f"x_unit{u}") for u in range(UNITS)]
+        x_unit = [held.tile([P, CB, width], F32, name=f"x_unit{u}") for u, width in enumerate(UNIT_WIDTHS)]
         z_piece = [held.tile([P, CB, width], BF16, name=f"z_piece{i}") for i, width in enumerate(WIDTHS)]
         x_whole = [held.tile([P, N], F32, name=f"x_whole{cb}") for cb in range(CB)]
         y_whole = [held.tile([P, N], F32, name=f"y_whole{cb}") for cb in range(CB)]
         window = [held.tile([P, S], F32, name=f"window{cb}") for cb in range(CB)]
         offsets = held.tile([P, N // 16], U16, name="offsets")
         hid = [[held.tile([P, BANK], BF16, name=f"hid{t}_{fb}") for fb in range(FB)] for t in range(N // BANK)]
-        w1_sb = [held.tile([P, CB, FH], BF16, name=f"w1_sb{h}") for h in range(HALVES)]
-        mask_sb = [held.tile([P, CB, FH], BF16, name=f"mask_sb{h}") for h in range(HALVES)]
-        w1m = [held.tile([P, CB, FH], BF16, name=f"w1m{h}") for h in range(HALVES)]
+        w1_sb = [held.tile([P, CB, FQ], BF16, name=f"w1_sb{q}") for q in range(QUARTERS)]
+        mask_sb = [held.tile([P, CB, FQ], BF16, name=f"mask_sb{q}") for q in range(QUARTERS)]
+        w1m = [held.tile([P, CB, FQ], BF16, name=f"w1m{q}") for q in range(QUARTERS)]
         w2_sb = held.tile([P, FB, C], BF16, name="w2_sb")
         vec_rows = held.tile([P, P], F32, name="vec_rows")
         vec_cols = held.tile([P, VEC_ROWS], F32, name="vec_cols")
@@ -64,17 +67,22 @@ def tile_randomsparsetransformer_kernel(
         mask_blocks = mask1.rearrange("(cb p) f -> p cb f", p=P)
 
         def load_x_unit(u):
-            nc.sync.dma_start(x_unit[u][:], x_blocks[:, :, u * UNIT : (u + 1) * UNIT])
+            nc.sync.dma_start(x_unit[u][:], x_blocks[:, :, UNIT_STARTS[u] : UNIT_STARTS[u] + UNIT_WIDTHS[u]])
+
+        def load_weights(q):
+            nc.sync.dma_start(w1_sb[q][:], w1_blocks[:, :, q * FQ : (q + 1) * FQ])
+            nc.sync.dma_start(mask_sb[q][:], mask_blocks[:, :, q * FQ : (q + 1) * FQ])
 
         load_x_unit(0)
         for row, vec in ((GAIN_ROW, ln_gain), (LN_BIAS_ROW, ln_bias), (B1_ROW, b1), (B2_ROW, b2)):
             rows = vec.shape[0] // P
             nc.sync.dma_start(vec_rows[row : row + rows, :], vec.rearrange("(r p) o -> r (p o)", p=P))
         load_x_unit(1)
-        for h in range(HALVES):
-            nc.sync.dma_start(w1_sb[h][:], w1_blocks[:, :, h * FH : (h + 1) * FH])
-            nc.sync.dma_start(mask_sb[h][:], mask_blocks[:, :, h * FH : (h + 1) * FH])
-        for u in range(2, UNITS):
+        for q in range(QUARTERS):
+            load_weights(q)
+            if q < QUARTERS // 2:
+                load_x_unit(2 + q)
+        for u in range(2 + QUARTERS // 2, UNITS):
             load_x_unit(u)
         nc.sync.dma_start(w2_sb[:], w2.rearrange("(fb p) c -> p fb c", p=P))
         nc.sync.dma_start(offsets[:], offs)
@@ -87,29 +95,31 @@ def tile_randomsparsetransformer_kernel(
             return vec_cols[:, row : row + 1]
 
         with (
+            tc.tile_pool(name="stat_pool", bufs=STATS_AT_ONCE) as stat_pool,
             tc.psum_pool(name="y_pool", bufs=2) as y_pool,
             tc.psum_pool(name="flip_pool", bufs=3) as flip_pool,
             tc.psum_pool(name="hid_pool", bufs=3) as hid_pool,
         ):
 
             def standardise(u):
-                x_flipped = flip_pool.tile([P, TB, C], F32, name="x_flipped", tag="flip")
-                for tb in range(TB):
+                blocks = UNIT_WIDTHS[u] // P
+                x_flipped = flip_pool.tile([P, blocks, C], F32, name="x_flipped", tag="flip")
+                for tb in range(blocks):
                     for cb in range(CB):
                         nc.tensor.transpose(
                             x_flipped[:, tb, cb * P : (cb + 1) * P],
                             x_unit[u][:, cb, tb * P : (tb + 1) * P],
                             identity[:],
                         )
-                stats = work.tile([P, TB, 6], F32, name="stats")
-                mean_var = work.tile([P, TB, 2], F32, name="mean_var")
-                for tb in range(TB):
-                    nc.vector.bn_stats(stats[:, tb, :], x_flipped[:, tb, :])
-                    nc.vector.bn_aggr(mean_var[:, tb, :], stats[:, tb, :])
-                rstd = work.tile([P, TB], F32, name="rstd")
+                stats = stat_pool.tile([P, blocks, 8], F32, name="stats", tag="stats")
+                mean_var = stats[:, :, 6:8]
+                for tb in range(blocks):
+                    nc.vector.bn_stats(stats[:, tb, 0:6], x_flipped[:, tb, :])
+                    nc.vector.bn_aggr(mean_var[:, tb, :], stats[:, tb, 0:6])
+                rstd = work.tile([P, blocks], F32, name="rstd", tag="rstd")
                 nc.scalar.activation(rstd[:], mean_var[:, :, 1], ACT.Abs_reciprocal_sqrt, bias=eps_col[:])
-                standard = work.tile([P, TB, C], F32, name="standard")
-                for tb in range(TB):
+                standard = work.tile([P, blocks, C], F32, name="standard", tag="standard")
+                for tb in range(blocks):
                     nc.vector.tensor_scalar(
                         standard[:, tb, :],
                         x_flipped[:, tb, :],
@@ -121,14 +131,14 @@ def tile_randomsparsetransformer_kernel(
                 return standard
 
             def z_columns(u, cb):
-                i = max(i for i, (start, width) in enumerate(PIECES) if start <= u * UNIT)
-                first = u * UNIT - PIECES[i][0]
-                return z_piece[i][:, cb, first : first + UNIT]
+                i = max(i for i, (start, width) in enumerate(PIECES) if start <= UNIT_STARTS[u])
+                first = UNIT_STARTS[u] - PIECES[i][0]
+                return z_piece[i][:, cb, first : first + UNIT_WIDTHS[u]]
 
             def gain_and_bias(u, standard):
-                flipped_back = flip_pool.tile([P, CB, UNIT], F32, name="flipped_back", tag="flip")
+                flipped_back = flip_pool.tile([P, CB, UNIT_WIDTHS[u]], F32, name="flipped_back", tag="flip")
                 for cb in range(CB):
-                    for tb in range(TB):
+                    for tb in range(UNIT_WIDTHS[u] // P):
                         nc.tensor.transpose(
                             flipped_back[:, cb, tb * P : (tb + 1) * P],
                             standard[:, tb, cb * P : (cb + 1) * P],
@@ -143,19 +153,22 @@ def tile_randomsparsetransformer_kernel(
                         scale=column(GAIN_ROW + cb),
                     )
 
-            def mask_weights(h):
-                nc.gpsimd.tensor_tensor(w1m[h][:], w1_sb[h][:], mask_sb[h][:], ALU.mult)
+            def mask_weights(q):
+                nc.gpsimd.tensor_tensor(w1m[q][:], w1_sb[q][:], mask_sb[q][:], ALU.mult)
 
             def first_layer(i, hidden_blocks):
                 start, width = PIECES[i]
                 t, first = divmod(start, BANK)
                 for fb in hidden_blocks:
-                    h, first_in_half = divmod(fb * P, FH)
-                    hid_ps = hid_pool.tile([P, width], F32, name="hid_ps")
+                    q, first_in_quarter = divmod(fb * P, FQ)
+                    if width < BANK and fb % 2 == 0:
+                        hid_ps = y_pool.tile([P, width], F32, name="hid_ps", tag="y_ps")
+                    else:
+                        hid_ps = hid_pool.tile([P, width], F32, name="hid_ps", tag="hid_ps")
                     for cb in range(CB):
                         nc.tensor.matmul(
                             hid_ps[:],
-                            w1m[h][:, cb, first_in_half : first_in_half + P],
+                            w1m[q][:, cb, first_in_quarter : first_in_quarter + P],
                             z_piece[i][:, cb, :],
                             start=(cb == 0),
                             stop=(cb == CB - 1),
@@ -193,24 +206,35 @@ def tile_randomsparsetransformer_kernel(
                     standard[u + AHEAD] = standardise(u + AHEAD)
 
             standard[0] = standardise(0)
+            standard[1] = standardise(1)
             vec_ps = y_pool.tile([P, P], F32, name="vec_ps", tag="y_ps")
             nc.tensor.transpose(vec_ps[:], vec_rows[:], identity[:])
             nc.vector.tensor_copy(vec_cols[:], vec_ps[:, :VEC_ROWS])
-            mask_weights(0)
-            standard[1] = standardise(1)
-            mask_weights(1)
-            norm_step(0)
-            norm_step(1)
+            for q in range(QUARTERS):
+                mask_weights(q)
+            standard[2] = standardise(2)
+            gain_and_bias(0, standard[0])
+            gain_and_bias(1, standard[1])
 
-            next_unit = 2
-            for i, (start, width) in enumerate(PIECES):
-                parts = width // UNIT
-                for part in range(parts):
-                    first_layer(i, range(part * FB // parts, (part + 1) * FB // parts))
+            first_half, second_half = range(FB // 2), range(FB // 2, FB)
+            first_layer(0, first_half)
+            standard[3] = standardise(3)
+            gain_and_bias(2, standard[2])
+            standard[4] = standardise(4)
+            first_layer(1, first_half)
+            first_layer(0, second_half)
+            norm_step(3)
+            first_layer(1, second_half)
+            norm_step(4)
+            second_layer(0, 0)
+
+            next_unit = 5
+            for i, (start, width) in list(enumerate(PIECES))[2:]:
+                for half in (first_half, second_half):
+                    first_layer(i, half)
                     norm_step(next_unit)
                     next_unit += 1
-                if (start + width) % BANK == 0:
-                    second_layer(0, start // BANK)
+                second_layer(0, start // BANK)
             scatter(0)
             for t in range(N // BANK):
                 second_layer(1, t)

@@ -96,9 +96,9 @@ def tile_randomsparsetransformer_kernel(
 
         with (
             tc.tile_pool(name="stat_pool", bufs=STATS_AT_ONCE) as stat_pool,
-            tc.psum_pool(name="y_pool", bufs=2) as y_pool,
+            tc.psum_pool(name="y_pool", bufs=1) as y_pool,
             tc.psum_pool(name="flip_pool", bufs=3) as flip_pool,
-            tc.psum_pool(name="hid_pool", bufs=3) as hid_pool,
+            tc.psum_pool(name="hid_pool", bufs=4) as hid_pool,
         ):
 
             def standardise(u):
@@ -161,10 +161,7 @@ def tile_randomsparsetransformer_kernel(
                 t, first = divmod(start, BANK)
                 for fb in hidden_blocks:
                     q, first_in_quarter = divmod(fb * P, FQ)
-                    if width < BANK and fb % 2 == 0:
-                        hid_ps = y_pool.tile([P, width], F32, name="hid_ps", tag="y_ps")
-                    else:
-                        hid_ps = hid_pool.tile([P, width], F32, name="hid_ps", tag="hid_ps")
+                    hid_ps = hid_pool.tile([P, width], F32, name="hid_ps", tag="hid_ps")
                     for cb in range(CB):
                         nc.tensor.matmul(
                             hid_ps[:],
@@ -179,8 +176,8 @@ def tile_randomsparsetransformer_kernel(
                     else:
                         nc.vector.tensor_scalar(hid_out, hid_ps[:], column(B1_ROW + fb), 0.0, ALU.add, ALU.max)
 
-            def second_layer(cb, t):
-                y_ps = y_pool.tile([P, BANK], F32, name="y_ps")
+            def second_layer(cb, t, pool, tag):
+                y_ps = pool.tile([P, BANK], F32, name="y_ps", tag=tag)
                 for fb in range(FB):
                     nc.tensor.matmul(
                         y_ps[:],
@@ -226,7 +223,7 @@ def tile_randomsparsetransformer_kernel(
             norm_step(3)
             first_layer(1, second_half)
             norm_step(4)
-            second_layer(0, 0)
+            second_layer(0, 0, y_pool, "y_ps")
 
             next_unit = 5
             for i, (start, width) in list(enumerate(PIECES))[2:]:
@@ -234,8 +231,8 @@ def tile_randomsparsetransformer_kernel(
                     first_layer(i, half)
                     norm_step(next_unit)
                     next_unit += 1
-                second_layer(0, start // BANK)
+                second_layer(0, start // BANK, y_pool, "y_ps")
             scatter(0)
             for t in range(N // BANK):
-                second_layer(1, t)
+                second_layer(1, t, hid_pool, "hid_ps")
             scatter(1)

@@ -96,9 +96,8 @@ def tile_randomsparsetransformer_kernel(
 
         with (
             tc.tile_pool(name="stat_pool", bufs=STATS_AT_ONCE) as stat_pool,
-            tc.psum_pool(name="y_pool", bufs=1) as y_pool,
             tc.psum_pool(name="flip_pool", bufs=3) as flip_pool,
-            tc.psum_pool(name="hid_pool", bufs=4) as hid_pool,
+            tc.psum_pool(name="layer_pool", bufs=5) as layer_pool,
         ):
 
             def standardise(u):
@@ -161,7 +160,7 @@ def tile_randomsparsetransformer_kernel(
                 t, first = divmod(start, BANK)
                 for fb in hidden_blocks:
                     q, first_in_quarter = divmod(fb * P, FQ)
-                    hid_ps = hid_pool.tile([P, width], F32, name="hid_ps", tag="hid_ps")
+                    hid_ps = layer_pool.tile([P, width], F32, name="hid_ps", tag="layer")
                     for cb in range(CB):
                         nc.tensor.matmul(
                             hid_ps[:],
@@ -176,8 +175,8 @@ def tile_randomsparsetransformer_kernel(
                     else:
                         nc.vector.tensor_scalar(hid_out, hid_ps[:], column(B1_ROW + fb), 0.0, ALU.add, ALU.max)
 
-            def second_layer(cb, t, pool, tag):
-                y_ps = pool.tile([P, BANK], F32, name="y_ps", tag=tag)
+            def second_layer(cb, t):
+                y_ps = layer_pool.tile([P, BANK], F32, name="y_ps", tag="layer")
                 for fb in range(FB):
                     nc.tensor.matmul(
                         y_ps[:],
@@ -204,7 +203,7 @@ def tile_randomsparsetransformer_kernel(
 
             standard[0] = standardise(0)
             standard[1] = standardise(1)
-            vec_ps = y_pool.tile([P, P], F32, name="vec_ps", tag="y_ps")
+            vec_ps = layer_pool.tile([P, P], F32, name="vec_ps", tag="layer")
             nc.tensor.transpose(vec_ps[:], vec_rows[:], identity[:])
             nc.vector.tensor_copy(vec_cols[:], vec_ps[:, :VEC_ROWS])
             for q in range(QUARTERS):
@@ -223,7 +222,7 @@ def tile_randomsparsetransformer_kernel(
             norm_step(3)
             first_layer(1, second_half)
             norm_step(4)
-            second_layer(0, 0, y_pool, "y_ps")
+            second_layer(0, 0)
 
             next_unit = 5
             for i, (start, width) in list(enumerate(PIECES))[2:]:
@@ -231,8 +230,8 @@ def tile_randomsparsetransformer_kernel(
                     first_layer(i, half)
                     norm_step(next_unit)
                     next_unit += 1
-                second_layer(0, start // BANK, y_pool, "y_ps")
+                second_layer(0, start // BANK)
             scatter(0)
             for t in range(N // BANK):
-                second_layer(1, t, hid_pool, "hid_ps")
+                second_layer(1, t)
             scatter(1)

@@ -100,16 +100,19 @@ def tile_randomsparsetransformer_kernel(
             tc.psum_pool(name="layer_pool", bufs=5) as layer_pool,
         ):
 
-            def standardise(u):
+            def flip(u):
                 blocks = UNIT_WIDTHS[u] // P
                 x_flipped = flip_pool.tile([P, blocks, C], F32, name="x_flipped", tag="flip")
-                for tb in range(blocks):
-                    for cb in range(CB):
-                        nc.tensor.transpose(
-                            x_flipped[:, tb, cb * P : (cb + 1) * P],
-                            x_unit[u][:, cb, tb * P : (tb + 1) * P],
-                            identity[:],
-                        )
+
+                def one(tb, cb):
+                    nc.tensor.transpose(
+                        x_flipped[:, tb, cb * P : (cb + 1) * P], x_unit[u][:, cb, tb * P : (tb + 1) * P], identity[:]
+                    )
+
+                return x_flipped, [lambda tb=tb, cb=cb: one(tb, cb) for tb in range(blocks) for cb in range(CB)]
+
+            def normalise(u, x_flipped):
+                blocks = UNIT_WIDTHS[u] // P
                 stats = stat_pool.tile([P, blocks, 8], F32, name="stats", tag="stats")
                 mean_var = stats[:, :, 6:8]
                 for tb in range(blocks):
@@ -134,15 +137,31 @@ def tile_randomsparsetransformer_kernel(
                 first = UNIT_STARTS[u] - PIECES[i][0]
                 return z_piece[i][:, cb, first : first + UNIT_WIDTHS[u]]
 
-            def gain_and_bias(u, standard):
+            def standardise(u):
+                x_flipped, flips = flip(u)
+                for one_flip in flips:
+                    one_flip()
+                return normalise(u, x_flipped)
+
+            def flip_back(u, standard):
                 flipped_back = flip_pool.tile([P, CB, UNIT_WIDTHS[u]], F32, name="flipped_back", tag="flip")
-                for cb in range(CB):
-                    for tb in range(UNIT_WIDTHS[u] // P):
-                        nc.tensor.transpose(
-                            flipped_back[:, cb, tb * P : (tb + 1) * P],
-                            standard[:, tb, cb * P : (cb + 1) * P],
-                            identity[:],
-                        )
+
+                def one(cb, tb):
+                    nc.tensor.transpose(
+                        flipped_back[:, cb, tb * P : (tb + 1) * P], standard[:, tb, cb * P : (cb + 1) * P], identity[:]
+                    )
+
+                return flipped_back, [
+                    lambda cb=cb, tb=tb: one(cb, tb) for cb in range(CB) for tb in range(UNIT_WIDTHS[u] // P)
+                ]
+
+            def gain_and_bias(u, standard):
+                flipped_back, flips = flip_back(u, standard)
+                for one_flip in flips:
+                    one_flip()
+                write_z(u, flipped_back)
+
+            def write_z(u, flipped_back):
                 for cb in range(CB):
                     nc.scalar.activation(
                         z_columns(u, cb),
@@ -155,10 +174,10 @@ def tile_randomsparsetransformer_kernel(
             def mask_weights(q):
                 nc.gpsimd.tensor_tensor(w1m[q][:], w1_sb[q][:], mask_sb[q][:], ALU.mult)
 
-            def first_layer(i, hidden_blocks):
+            def first_layer(i, hidden_blocks, between=()):
                 start, width = PIECES[i]
                 t, first = divmod(start, BANK)
-                for fb in hidden_blocks:
+                for n, fb in enumerate(hidden_blocks):
                     q, first_in_quarter = divmod(fb * P, FQ)
                     hid_ps = layer_pool.tile([P, width], F32, name="hid_ps", tag="layer")
                     for cb in range(CB):
@@ -169,13 +188,15 @@ def tile_randomsparsetransformer_kernel(
                             start=(cb == 0),
                             stop=(cb == CB - 1),
                         )
+                        if n * CB + cb < len(between):
+                            between[n * CB + cb]()
                     hid_out = hid[t][fb][:, first : first + width]
                     if fb % 4 != 3:
                         nc.scalar.activation(hid_out, hid_ps[:], ACT.Relu, bias=column(B1_ROW + fb))
                     else:
                         nc.vector.tensor_scalar(hid_out, hid_ps[:], column(B1_ROW + fb), 0.0, ALU.add, ALU.max)
 
-            def second_layer(cb, t):
+            def second_layer(cb, t, between=()):
                 y_ps = layer_pool.tile([P, BANK], F32, name="y_ps", tag="layer")
                 for fb in range(FB):
                     nc.tensor.matmul(
@@ -185,6 +206,8 @@ def tile_randomsparsetransformer_kernel(
                         start=(fb == 0),
                         stop=(fb == FB - 1),
                     )
+                    if fb < len(between):
+                        between[fb]()
                 nc.scalar.activation(
                     y_whole[cb][:, t * BANK : (t + 1) * BANK], y_ps[:], ACT.Identity, bias=column(B2_ROW + cb)
                 )
@@ -200,6 +223,26 @@ def tile_randomsparsetransformer_kernel(
                     gain_and_bias(u, standard[u])
                 if u + AHEAD < UNITS:
                     standard[u + AHEAD] = standardise(u + AHEAD)
+
+            def step_calls(u):
+                calls = []
+                if u < UNITS:
+                    flipped_back, flips = flip_back(u, standard[u])
+
+                    def last_back():
+                        flips[-1]()
+                        write_z(u, flipped_back)
+
+                    calls += flips[:-1] + [last_back]
+                if u + AHEAD < UNITS:
+                    x_flipped, flips_in = flip(u + AHEAD)
+
+                    def last_in():
+                        flips_in[-1]()
+                        standard[u + AHEAD] = normalise(u + AHEAD, x_flipped)
+
+                    calls += flips_in[:-1] + [last_in]
+                return calls
 
             standard[0] = standardise(0)
             standard[1] = standardise(1)
@@ -226,11 +269,10 @@ def tile_randomsparsetransformer_kernel(
 
             next_unit = 5
             for i, (start, width) in list(enumerate(PIECES))[2:]:
-                for half in (first_half, second_half):
-                    first_layer(i, half)
-                    norm_step(next_unit)
-                    next_unit += 1
-                second_layer(0, start // BANK)
+                first_layer(i, first_half)
+                first_layer(i, second_half, step_calls(next_unit))
+                second_layer(0, start // BANK, step_calls(next_unit + 1))
+                next_unit += 2
             scatter(0)
             for t in range(N // BANK):
                 second_layer(1, t)

@@ -74,15 +74,17 @@ def tile_randomsparsetransformer_kernel(
             nc.sync.dma_start(mask_sb[q][:], mask_blocks[:, :, q * FQ : (q + 1) * FQ])
 
         load_x_unit(0)
+        load_x_unit(1)
+        load_weights(0)
+        load_x_unit(2)
         for row, vec in ((GAIN_ROW, ln_gain), (LN_BIAS_ROW, ln_bias), (B1_ROW, b1), (B2_ROW, b2)):
             rows = vec.shape[0] // P
             nc.sync.dma_start(vec_rows[row : row + rows, :], vec.rearrange("(r p) o -> r (p o)", p=P))
-        load_x_unit(1)
-        for q in range(QUARTERS):
+        for q in range(1, QUARTERS):
             load_weights(q)
-            if q < QUARTERS // 2:
-                load_x_unit(2 + q)
-        for u in range(2 + QUARTERS // 2, UNITS):
+            if q == 2:
+                load_x_unit(3)
+        for u in range(4, UNITS):
             load_x_unit(u)
         nc.sync.dma_start(w2_sb[:], w2.rearrange("(fb p) c -> p fb c", p=P))
         nc.sync.dma_start(offsets[:], offs)
@@ -100,9 +102,9 @@ def tile_randomsparsetransformer_kernel(
             tc.psum_pool(name="layer_pool", bufs=5) as layer_pool,
         ):
 
-            def flip(u):
+            def flip(u, pool=flip_pool, tag="flip"):
                 blocks = UNIT_WIDTHS[u] // P
-                x_flipped = flip_pool.tile([P, blocks, C], F32, name="x_flipped", tag="flip")
+                x_flipped = pool.tile([P, blocks, C], F32, name="x_flipped", tag=tag)
 
                 def one(tb, cb):
                     nc.tensor.transpose(
@@ -138,7 +140,7 @@ def tile_randomsparsetransformer_kernel(
                 return z_piece[i][:, cb, first : first + UNIT_WIDTHS[u]]
 
             def standardise(u):
-                x_flipped, flips = flip(u)
+                x_flipped, flips = flip(u, layer_pool, "layer")
                 for one_flip in flips:
                     one_flip()
                 return normalise(u, x_flipped)
@@ -218,54 +220,49 @@ def tile_randomsparsetransformer_kernel(
 
             standard = {}
 
-            def norm_step(u):
-                if u < UNITS:
-                    gain_and_bias(u, standard[u])
-                if u + AHEAD < UNITS:
-                    standard[u + AHEAD] = standardise(u + AHEAD)
+            def back_calls(u):
+                if u >= UNITS:
+                    return []
+                flipped_back, flips = flip_back(u, standard[u])
+
+                def last():
+                    flips[-1]()
+                    write_z(u, flipped_back)
+
+                return flips[:-1] + [last]
+
+            def in_calls(u):
+                if u >= UNITS:
+                    return []
+                x_flipped, flips = flip(u)
+
+                def last():
+                    flips[-1]()
+                    standard[u] = normalise(u, x_flipped)
+
+                return flips[:-1] + [last]
 
             def step_calls(u):
-                calls = []
-                if u < UNITS:
-                    flipped_back, flips = flip_back(u, standard[u])
-
-                    def last_back():
-                        flips[-1]()
-                        write_z(u, flipped_back)
-
-                    calls += flips[:-1] + [last_back]
-                if u + AHEAD < UNITS:
-                    x_flipped, flips_in = flip(u + AHEAD)
-
-                    def last_in():
-                        flips_in[-1]()
-                        standard[u + AHEAD] = normalise(u + AHEAD, x_flipped)
-
-                    calls += flips_in[:-1] + [last_in]
-                return calls
+                return back_calls(u) + in_calls(u + AHEAD)
 
             standard[0] = standardise(0)
             standard[1] = standardise(1)
+            standard[2] = standardise(2)
             vec_ps = layer_pool.tile([P, P], F32, name="vec_ps", tag="layer")
             nc.tensor.transpose(vec_ps[:], vec_rows[:], identity[:])
             nc.vector.tensor_copy(vec_cols[:], vec_ps[:, :VEC_ROWS])
             for q in range(QUARTERS):
                 mask_weights(q)
-            standard[2] = standardise(2)
             gain_and_bias(0, standard[0])
             gain_and_bias(1, standard[1])
 
+            early, late = range(FB - FB // QUARTERS), range(FB - FB // QUARTERS, FB)
             first_half, second_half = range(FB // 2), range(FB // 2, FB)
-            first_layer(0, first_half)
-            standard[3] = standardise(3)
-            gain_and_bias(2, standard[2])
-            standard[4] = standardise(4)
-            first_layer(1, first_half)
-            first_layer(0, second_half)
-            norm_step(3)
-            first_layer(1, second_half)
-            norm_step(4)
-            second_layer(0, 0)
+            first_layer(0, early, in_calls(3) + back_calls(2))
+            first_layer(1, first_half, in_calls(4))
+            first_layer(0, late)
+            first_layer(1, second_half, step_calls(3))
+            second_layer(0, 0, step_calls(4))
 
             next_unit = 5
             for i, (start, width) in list(enumerate(PIECES))[2:]:

@@ -82,7 +82,7 @@ def tile_randomsparsetransformer_kernel(
             nc.sync.dma_start(vec_rows[row : row + rows, :], vec.rearrange("(r p) o -> r (p o)", p=P))
         for q in range(1, QUARTERS):
             load_weights(q)
-            if q == 2:
+            if q == 1:
                 load_x_unit(3)
         for u in range(4, UNITS):
             load_x_unit(u)
@@ -250,7 +250,7 @@ def tile_randomsparsetransformer_kernel(
             standard[2] = standardise(2)
             vec_ps = layer_pool.tile([P, P], F32, name="vec_ps", tag="layer")
             nc.tensor.transpose(vec_ps[:], vec_rows[:], identity[:])
-            nc.vector.tensor_copy(vec_cols[:], vec_ps[:, :VEC_ROWS])
+            nc.scalar.activation(vec_cols[:], vec_ps[:, :VEC_ROWS], ACT.Identity)
             for q in range(QUARTERS):
                 mask_weights(q)
             gain_and_bias(0, standard[0])

@@ -82,9 +82,9 @@ def tile_randomsparsetransformer_kernel(
             nc.sync.dma_start(vec_rows[row : row + rows, :], vec.rearrange("(r p) o -> r (p o)", p=P))
         for q in range(1, QUARTERS):
             load_weights(q)
-            if q == 1:
-                load_x_unit(3)
-        for u in range(4, UNITS):
+            if q < QUARTERS - 1:
+                load_x_unit(q + 2)
+        for u in range(QUARTERS + 1, UNITS):
             load_x_unit(u)
         nc.sync.dma_start(w2_sb[:], w2.rearrange("(fb p) c -> p fb c", p=P))
         nc.sync.dma_start(offsets[:], offs)

import concourse.mybir as mybir
from concourse.masks import make_identity

F32 = mybir.dt.float32
BF16 = mybir.dt.bfloat16
U16 = mybir.dt.uint16
ALU = mybir.AluOpType
ACT = mybir.ActivationFunctionType

P = 128
C, F, S, N = 256, 1024, 4096, 2048
CB = C // P
FB = F // P
BANK = 512
EPS = 1e-5

FLOPS = 2 * N * C * F * 2

WHOLE = BANK // C * P
UNIT_WIDTHS = [P, P] + [WHOLE] * ((N - 2 * P) // WHOLE)
assert sum(UNIT_WIDTHS) == N
UNITS = len(UNIT_WIDTHS)
UNIT_STARTS = [sum(UNIT_WIDTHS[:u]) for u in range(UNITS)]

WIDTHS = [WHOLE, WHOLE, BANK, BANK, BANK]
assert sum(WIDTHS) == N
PIECES = [(sum(WIDTHS[:i]), width) for i, width in enumerate(WIDTHS)]
assert all(start // BANK == (start + width - 1) // BANK for start, width in PIECES)
AHEAD = 2
IN_FLIGHT = AHEAD + 2
STATS_AT_ONCE = 2

QUARTERS = 4
FQ = F // QUARTERS

GAIN_ROW, LN_BIAS_ROW, B1_ROW, B2_ROW = 0, CB, 2 * CB, 2 * CB + FB
VEC_ROWS = 3 * CB + FB


def tile_randomsparsetransformer_kernel(
    tc, base, x, ln_gain, ln_bias, w1, mask1, b1, w2, b2, offs, out
):
    nc = tc.nc
    with tc.tile_pool(name="held", bufs=1) as held, tc.tile_pool(name="work", bufs=IN_FLIGHT) as work:
        x_unit = [held.tile([P, CB, width], F32, name=f"x_unit{u}") for u, width in enumerate(UNIT_WIDTHS)]
        z_piece = [held.tile([P, CB, width], BF16, name=f"z_piece{i}") for i, width in enumerate(WIDTHS)]
        x_whole = [held.tile([P, N], F32, name=f"x_whole{cb}") for cb in range(CB)]
        y_whole = [held.tile([P, N], F32, name=f"y_whole{cb}") for cb in range(CB)]
        window = [held.tile([P, S], F32, name=f"window{cb}") for cb in range(CB)]
        offsets = held.tile([P, N // 16], U16, name="offsets")
        hid = [[held.tile([P, BANK], BF16, name=f"hid{t}_{fb}") for fb in range(FB)] for t in range(N // BANK)]
        w1_sb = [held.tile([P, CB, FQ], BF16, name=f"w1_sb{q}") for q in range(QUARTERS)]
        mask_sb = [held.tile([P, CB, FQ], BF16, name=f"mask_sb{q}") for q in range(QUARTERS)]
        w1m = [held.tile([P, CB, FQ], BF16, name=f"w1m{q}") for q in range(QUARTERS)]
        w2_sb = held.tile([P, FB, C], BF16, name="w2_sb")
        vec_rows = held.tile([P, P], F32, name="vec_rows")
        vec_cols = held.tile([P, VEC_ROWS], F32, name="vec_cols")
        identity = held.tile([P, P], F32, name="identity")
        eps_col = held.tile([P, 1], F32, name="eps_col")

        nc.vector.memset(vec_rows[:], 0.0)
        nc.vector.memset(eps_col[:], EPS)
        make_identity(nc, identity[:])

        x_blocks = x.rearrange("(cb p) n -> p cb n", p=P)
        w1_blocks = w1.rearrange("(cb p) f -> p cb f", p=P)
        mask_blocks = mask1.rearrange("(cb p) f -> p cb f", p=P)

        def load_x_unit(u):
            nc.sync.dma_start(x_unit[u][:], x_blocks[:, :, UNIT_STARTS[u] : UNIT_STARTS[u] + UNIT_WIDTHS[u]])

        def load_weights(q):
            nc.sync.dma_start(w1_sb[q][:], w1_blocks[:, :, q * FQ : (q + 1) * FQ])
            nc.sync.dma_start(mask_sb[q][:], mask_blocks[:, :, q * FQ : (q + 1) * FQ])

        load_x_unit(0)
        load_x_unit(1)
        load_weights(0)
        load_x_unit(2)
        for row, vec in ((GAIN_ROW, ln_gain), (LN_BIAS_ROW, ln_bias), (B1_ROW, b1), (B2_ROW, b2)):
            rows = vec.shape[0] // P
            nc.sync.dma_start(vec_rows[row : row + rows, :], vec.rearrange("(r p) o -> r (p o)", p=P))
        for q in range(1, QUARTERS):
            load_weights(q)
            if q < QUARTERS - 1:
                load_x_unit(q + 2)
        for u in range(QUARTERS + 1, UNITS):
            load_x_unit(u)
        nc.sync.dma_start(w2_sb[:], w2.rearrange("(fb p) c -> p fb c", p=P))
        nc.sync.dma_start(offsets[:], offs)
        for cb in range(CB):
            nc.sync.dma_start(x_whole[cb][:], x[cb * P : (cb + 1) * P, :])
        for cb in range(CB):
            nc.sync.dma_start(window[cb][:], base[cb * P : (cb + 1) * P, :])

        def column(row):
            return vec_cols[:, row : row + 1]

        with (
            tc.tile_pool(name="stat_pool", bufs=STATS_AT_ONCE) as stat_pool,
            tc.psum_pool(name="flip_pool", bufs=3) as flip_pool,
            tc.psum_pool(name="layer_pool", bufs=5) as layer_pool,
        ):

            def flip(u, pool=flip_pool, tag="flip"):
                blocks = UNIT_WIDTHS[u] // P
                x_flipped = pool.tile([P, blocks, C], F32, name="x_flipped", tag=tag)

                def one(tb, cb):
                    nc.tensor.transpose(
                        x_flipped[:, tb, cb * P : (cb + 1) * P], x_unit[u][:, cb, tb * P : (tb + 1) * P], identity[:]
                    )

                return x_flipped, [lambda tb=tb, cb=cb: one(tb, cb) for tb in range(blocks) for cb in range(CB)]

            def normalise(u, x_flipped):
                blocks = UNIT_WIDTHS[u] // P
                stats = stat_pool.tile([P, blocks, 8], F32, name="stats", tag="stats")
                mean_var = stats[:, :, 6:8]
                for tb in range(blocks):
                    nc.vector.bn_stats(stats[:, tb, 0:6], x_flipped[:, tb, :])
                    nc.vector.bn_aggr(mean_var[:, tb, :], stats[:, tb, 0:6])
                rstd = work.tile([P, blocks], F32, name="rstd", tag="rstd")
                nc.scalar.activation(rstd[:], mean_var[:, :, 1], ACT.Abs_reciprocal_sqrt, bias=eps_col[:])
                standard = work.tile([P, blocks, C], F32, name="standard", tag="standard")
                for tb in range(blocks):
                    nc.vector.tensor_scalar(
                        standard[:, tb, :],
                        x_flipped[:, tb, :],
                        mean_var[:, tb, 0:1],
                        rstd[:, tb : tb + 1],
                        ALU.subtract,
                        ALU.mult,
                    )
                return standard

            def z_columns(u, cb):
                i = max(i for i, (start, width) in enumerate(PIECES) if start <= UNIT_STARTS[u])
                first = UNIT_STARTS[u] - PIECES[i][0]
                return z_piece[i][:, cb, first : first + UNIT_WIDTHS[u]]

            def standardise(u):
                x_flipped, flips = flip(u, layer_pool, "layer")
                for one_flip in flips:
                    one_flip()
                return normalise(u, x_flipped)

            def flip_back(u, standard):
                flipped_back = flip_pool.tile([P, CB, UNIT_WIDTHS[u]], F32, name="flipped_back", tag="flip")

                def one(cb, tb):
                    nc.tensor.transpose(
                        flipped_back[:, cb, tb * P : (tb + 1) * P], standard[:, tb, cb * P : (cb + 1) * P], identity[:]
                    )

                return flipped_back, [
                    lambda cb=cb, tb=tb: one(cb, tb) for cb in range(CB) for tb in range(UNIT_WIDTHS[u] // P)
                ]

            def gain_and_bias(u, standard):
                flipped_back, flips = flip_back(u, standard)
                for one_flip in flips:
                    one_flip()
                write_z(u, flipped_back)

            def write_z(u, flipped_back):
                for cb in range(CB):
                    nc.scalar.activation(
                        z_columns(u, cb),
                        flipped_back[:, cb, :],
                        ACT.Identity,
                        bias=column(LN_BIAS_ROW + cb),
                        scale=column(GAIN_ROW + cb),
                    )

            def mask_weights(q):
                nc.gpsimd.tensor_tensor(w1m[q][:], w1_sb[q][:], mask_sb[q][:], ALU.mult)

            def first_layer(i, hidden_blocks, between=()):
                start, width = PIECES[i]
                t, first = divmod(start, BANK)
                for n, fb in enumerate(hidden_blocks):
                    q, first_in_quarter = divmod(fb * P, FQ)
                    hid_ps = layer_pool.tile([P, width], F32, name="hid_ps", tag="layer")
                    for cb in range(CB):
                        nc.tensor.matmul(
                            hid_ps[:],
                            w1m[q][:, cb, first_in_quarter : first_in_quarter + P],
                            z_piece[i][:, cb, :],
                            start=(cb == 0),
                            stop=(cb == CB - 1),
                        )
                        if n * CB + cb < len(between):
                            between[n * CB + cb]()
                    hid_out = hid[t][fb][:, first : first + width]
                    if fb % 4 != 3:
                        nc.scalar.activation(hid_out, hid_ps[:], ACT.Relu, bias=column(B1_ROW + fb))
                    else:
                        nc.vector.tensor_scalar(hid_out, hid_ps[:], column(B1_ROW + fb), 0.0, ALU.add, ALU.max)

            def second_layer(cb, t, between=()):
                y_ps = layer_pool.tile([P, BANK], F32, name="y_ps", tag="layer")
                for fb in range(FB):
                    nc.tensor.matmul(
                        y_ps[:],
                        w2_sb[:, fb, cb * P : (cb + 1) * P],
                        hid[t][fb][:],
                        start=(fb == 0),
                        stop=(fb == FB - 1),
                    )
                    if fb < len(between):
                        between[fb]()
                nc.scalar.activation(
                    y_whole[cb][:, t * BANK : (t + 1) * BANK], y_ps[:], ACT.Identity, bias=column(B2_ROW + cb)
                )

            def scatter(cb):
                nc.vector.tensor_tensor(window[cb][:].indirect(offsets[:]), x_whole[cb][:], y_whole[cb][:], ALU.add)
                nc.sync.dma_start(out[cb * P : (cb + 1) * P, :], window[cb][:])

            standard = {}

            def back_calls(u):
                if u >= UNITS:
                    return []
                flipped_back, flips = flip_back(u, standard[u])

                def last():
                    flips[-1]()
                    write_z(u, flipped_back)

                return flips[:-1] + [last]

            def in_calls(u):
                if u >= UNITS:
                    return []
                x_flipped, flips = flip(u)

                def last():
                    flips[-1]()
                    standard[u] = normalise(u, x_flipped)

                return flips[:-1] + [last]

            def step_calls(u):
                return back_calls(u) + in_calls(u + AHEAD)

            standard[0] = standardise(0)
            standard[1] = standardise(1)
            standard[2] = standardise(2)
            vec_ps = layer_pool.tile([P, P], F32, name="vec_ps", tag="layer")
            nc.tensor.transpose(vec_ps[:], vec_rows[:], identity[:])
            nc.scalar.activation(vec_cols[:], vec_ps[:, :VEC_ROWS], ACT.Identity)
            for q in range(QUARTERS):
                mask_weights(q)
            gain_and_bias(0, standard[0])
            gain_and_bias(1, standard[1])

            early, late = range(FB - FB // QUARTERS), range(FB - FB // QUARTERS, FB)
            first_half, second_half = range(FB // 2), range(FB // 2, FB)
            first_layer(0, early, in_calls(3) + back_calls(2))
            first_layer(1, first_half, in_calls(4))
            first_layer(0, late)
            first_layer(1, second_half, step_calls(3))
            second_layer(0, 0, step_calls(4))

            next_unit = 5
            for i, (start, width) in list(enumerate(PIECES))[2:]:
                first_layer(i, first_half)
                first_layer(i, second_half, step_calls(next_unit))
                second_layer(0, start // BANK, step_calls(next_unit + 1))
                next_unit += 2
            scatter(0)
            for t in range(N // BANK):
                second_layer(1, t)
            scatter(1)
